import numpy as np
import ml_dtypes


def mxq(x, axis, fmt="e4m3"):
    dtype, down = {"e4m3": (ml_dtypes.float8_e4m3fn, 7), "e5m2": (ml_dtypes.float8_e5m2, 14)}[fmt]
    v = np.moveaxis(np.asarray(x, np.float32).astype(ml_dtypes.bfloat16).astype(np.float64), axis, -1)
    blocks = v.reshape(v.shape[:-1] + (-1, 32))
    amax = np.abs(blocks).max(-1, keepdims=True)
    byte = np.maximum(np.where(amax > 0, np.frexp(amax)[1] - 1 + 127, 0) - down, 1)
    scale = np.exp2(byte - 127.0)
    codes = (blocks / scale).astype(np.float32).astype(dtype).astype(np.float64)
    return np.moveaxis((codes * scale).reshape(v.shape), -1, axis)


WIDE = False


def mx_kscale(k):
    if not WIDE:
        return np.ones(k)
    levels = np.array([10, -10, 5, -5, 0])
    a = np.random.permutation(np.resize(levels, k // 512 * 4)).reshape(k // 512, 4)
    idx = np.arange(k)
    return np.exp2(a[idx // 512, idx % 128 // 32])


BF16 = ml_dtypes.bfloat16


def bf(x):
    return np.asarray(x, np.float32).astype(BF16)


def f64(x):
    return np.asarray(x).astype(np.float64)


B, D_IN, D_OUT = 128, 1024, 1024
EPS = 0.01


def setup_inputs():
    s, t = mx_kscale(D_IN), mx_kscale(D_OUT)
    return {"x": bf(np.random.standard_normal((B, D_IN)) * s),
            "W": bf(np.random.standard_normal((D_OUT, D_IN)) / np.sqrt(D_IN) / s[None, :] * t[:, None]),
            "b": bf(np.random.standard_normal(D_OUT) * 0.3 * t),
            "g": bf(np.random.standard_normal((D_OUT, D_OUT)) / np.sqrt(D_OUT) / t[None, :]),
            "g_bias": bf(np.random.standard_normal(D_OUT) * 0.3)}


def reference(x, W, b, g, g_bias):
    h = (mxq(f64(x), 1, "e4m3") @ mxq(f64(W), 1, "e4m3").T) + f64(b)
    c = np.cos((mxq(h, 1, "e4m3") @ mxq(f64(g), 1, "e4m3").T) + f64(g_bias))
    return np.where(np.abs(c) < EPS, -c, c)

@@ -1,0 +1,218 @@
+import math
+from contextlib import ExitStack
+
+import concourse.mybir as mybir
+from concourse.masks import make_identity
+
+F32 = mybir.dt.float32
+BF16 = mybir.dt.bfloat16
+U32 = mybir.dt.uint32
+U8 = mybir.dt.uint8
+FP8X4 = mybir.dt.float8_e4m3fn_x4
+ALU = mybir.AluOpType
+ACT = mybir.ActivationFunctionType
+
+P = 128
+PACK = 4
+K_PASS = P * PACK
+BATCH = 128
+D = 1024
+PASSES = D // K_PASS
+CHUNKS = D // P
+PAIRS = CHUNKS // 2
+PAIR_ROWS = 2 * P
+ROW_WORDS = D // 2
+PAIR_CODES = PASSES * PAIR_ROWS
+BANK = 512
+
+EPS = 0.01
+TURN = 2.0 * math.pi
+ROUND = 1.5 * 2.0**23
+
+FLOPS = 2 * 2 * BATCH * D * D
+
+
+def tile_onehiddenlayer_s_kernel(tc, x, W, b, g, g_bias, out):
+    nc = tc.nc
+    with ExitStack() as ctx:
+        keep = ctx.enter_context(tc.tile_pool(name="keep", bufs=1))
+        work = ctx.enter_context(tc.tile_pool(name="work", bufs=PAIRS))
+        psum_turned = ctx.enter_context(tc.psum_pool(name="psum_turned", bufs=4))
+        psum_h = ctx.enter_context(tc.psum_pool(name="psum_h", bufs=PASSES))
+        psum_z = ctx.enter_context(tc.psum_pool(name="psum_z", bufs=2))
+
+        x_rows = keep.tile([P, D], BF16)
+        w_rows = keep.tile([P, CHUNKS * D], BF16)
+        g_rows = keep.tile([P, CHUNKS * D], BF16)
+        x_grouped = keep.tile([P, D], BF16, align_bytes=64)
+        w_grouped = keep.tile([P, CHUNKS * D], BF16, align_bytes=64)
+        g_grouped = keep.tile([P, CHUNKS * D], BF16, align_bytes=64)
+        h_grouped = keep.tile([P, D], BF16, align_bytes=64)
+        x_codes = keep.tile([P, PASSES * BATCH], U32, align_bytes=64)
+        x_scales = keep.tile([P, PASSES * BATCH], U8, align_bytes=64)
+        w_codes = keep.tile([P, PAIRS * PAIR_CODES], U32, align_bytes=64)
+        w_scales = keep.tile([P, PAIRS * PAIR_CODES], U8, align_bytes=64)
+        g_codes = keep.tile([P, PAIRS * PAIR_CODES], U32, align_bytes=64)
+        g_scales = keep.tile([P, PAIRS * PAIR_CODES], U8, align_bytes=64)
+        h_codes = keep.tile([P, PASSES * BATCH], U32, align_bytes=64)
+        h_scales = keep.tile([P, PASSES * BATCH], U8, align_bytes=64)
+
+        ident = keep.tile([P, P], F32)
+        ones = keep.tile([P, P], BF16)
+        b_as_rows = keep.tile([P, PAIR_ROWS], BF16)
+        g_bias_as_row = keep.tile([P, D], BF16)
+        b_by_partition = keep.tile([P, CHUNKS], F32)
+        g_bias_turns = keep.tile([P, D], F32)
+        zero_column = keep.tile([P, 1], F32)
+        sine_of_zero = keep.tile([P, 1], F32)
+
+        nc.vector.memset(zero_column[:], 0.0)
+        nc.vector.memset(b_as_rows[:], 0.0)
+        nc.vector.memset(g_bias_as_row[:], 0.0)
+        nc.vector.memset(ones[:], 1.0)
+        make_identity(nc, ident[:])
+        nc.scalar.dma_start(out=b_as_rows[0:PAIRS, :], in_=b.rearrange("(a q) -> a q", a=PAIRS))
+        nc.scalar.dma_start(out=g_bias_as_row[0:1, :], in_=g_bias.rearrange("(o n) -> o n", o=1))
+        nc.scalar.activation(out=sine_of_zero[:], in_=zero_column[:], func=ACT.Sin)
+
+        nc.sync.dma_start(out=x_rows[:], in_=x)
+        w_pairs = W.rearrange("(a p e) k -> a p (e k)", p=P, e=2)
+        for a in range(PAIRS):
+            nc.sync.dma_start(out=w_rows[:, a * 2 * D : (a + 1) * 2 * D], in_=w_pairs[a])
+        for i in range(CHUNKS):
+            nc.sync.dma_start(out=g_rows[:, i * D : (i + 1) * D], in_=g[i * P : (i + 1) * P, :])
+
+        def turn_chunk(row_words, grouped_words, on_vector):
+            turned = psum_turned.tile([P, PASSES, 2, P], F32)
+            for s in range(PASSES):
+                for u in range(2):
+                    first = (2 * s + u) * P
+                    nc.tensor.transpose(turned[:, s, u, :], row_words[:, first : first + P], ident[:])
+            side_by_side = turned[:].rearrange("p s u r -> p s r u")
+            if on_vector:
+                nc.vector.tensor_copy(out=grouped_words, in_=side_by_side)
+            else:
+                nc.scalar.copy(out=grouped_words, in_=side_by_side)
+
+        def turn_pair(rows, grouped, a, vector_takes_second):
+            row_words = rows[:].bitcast(F32)
+            grouped_words = grouped[:].bitcast(F32).rearrange(
+                "p (a s r u) -> p a s r u", a=PAIRS, s=PASSES, r=PAIR_ROWS, u=2
+            )
+            for e in range(2):
+                i = 2 * a + e
+                turn_chunk(
+                    row_words[:, i * ROW_WORDS : (i + 1) * ROW_WORDS],
+                    grouped_words[:, a, :, e * P : (e + 1) * P, :],
+                    on_vector=(vector_takes_second and e == 1),
+                )
+
+        def quantise_pair(grouped, codes, scales, a):
+            nc.vector.quantize_mx(
+                out=codes[:, a * PAIR_CODES : (a + 1) * PAIR_CODES].bitcast(FP8X4),
+                scales=scales[:, a * PAIR_CODES : (a + 1) * PAIR_CODES],
+                in_=grouped[:, a * PAIR_CODES * PACK : (a + 1) * PAIR_CODES * PACK],
+            )
+
+        turn_chunk(
+            x_rows[:].bitcast(F32),
+            x_grouped[:].bitcast(F32).rearrange("p (s r u) -> p s r u", s=PASSES, r=BATCH, u=2),
+            on_vector=True,
+        )
+        nc.vector.quantize_mx(out=x_codes[:].bitcast(FP8X4), scales=x_scales[:], in_=x_grouped[:])
+
+        b_turned = psum_turned.tile([P, P], F32, tag="turned")
+        nc.tensor.transpose(b_turned[:], b_as_rows[:].bitcast(F32), ident[:])
+        nc.vector.tensor_copy(out=b_by_partition[:], in_=b_turned[:].bitcast(BF16)[:, 0:CHUNKS])
+
+        for half in range(D // BANK):
+            cols = slice(half * BANK, (half + 1) * BANK)
+            spread = psum_z.tile([P, BANK], F32, tag="z")
+            nc.tensor.matmul(out=spread[:], lhsT=ones[:], rhs=g_bias_as_row[:, cols], start=True, stop=True)
+            nc.vector.tensor_scalar(
+                out=g_bias_turns[:, cols], in0=spread[:],
+                scalar1=1.0 / TURN, scalar2=0.25, op0=ALU.mult, op1=ALU.add,
+            )
+
+        for a in range(PAIRS):
+            turn_pair(w_rows, w_grouped, a, vector_takes_second=(a % 2 == 1))
+            quantise_pair(w_grouped, w_codes, w_scales, a)
+
+        h_by_pass = h_grouped[:].rearrange("p (s r t) -> p s r t", s=PASSES, r=BATCH, t=PACK)
+        for s2 in range(PASSES):
+            h_turned = psum_h.tile([P, PACK, BATCH], F32)
+            for t in range(PACK):
+                i = s2 * PACK + t
+                for s in range(PASSES):
+                    w_cols = slice(
+                        (i // 2) * PAIR_CODES + s * PAIR_ROWS + (i % 2) * P,
+                        (i // 2) * PAIR_CODES + s * PAIR_ROWS + (i % 2) * P + P,
+                    )
+                    x_cols = slice(s * BATCH, (s + 1) * BATCH)
+                    nc.tensor.matmul_mx(
+                        out=h_turned[:, t, :],
+                        lhsT=w_codes[:, w_cols].bitcast(FP8X4),
+                        lhsT_scale=w_scales[:, w_cols],
+                        rhs=x_codes[:, x_cols].bitcast(FP8X4),
+                        rhs_scale=x_scales[:, x_cols],
+                        start=(s == 0),
+                        stop=(s == PASSES - 1),
+                    )
+            nc.vector.tensor_tensor(
+                out=h_by_pass[:, s2],
+                in0=h_turned[:].rearrange("p t r -> p r t"),
+                in1=b_by_partition[:, s2 * PACK : (s2 + 1) * PACK].unsqueeze(1).to_broadcast([P, BATCH, PACK]),
+                op=ALU.add,
+            )
+            nc.vector.quantize_mx(
+                out=h_codes[:, s2 * BATCH : (s2 + 1) * BATCH].bitcast(FP8X4),
+                scales=h_scales[:, s2 * BATCH : (s2 + 1) * BATCH],
+                in_=h_grouped[:, s2 * BATCH * PACK : (s2 + 1) * BATCH * PACK],
+            )
+
+        for a in range(PAIRS):
+            turn_pair(g_rows, g_grouped, a, vector_takes_second=False)
+            quantise_pair(g_grouped, g_codes, g_scales, a)
+
+            z = psum_z.tile([P, PAIR_ROWS], F32, tag="z")
+            for s in range(PASSES):
+                h_cols = slice(s * BATCH, (s + 1) * BATCH)
+                g_cols = slice(a * PAIR_CODES + s * PAIR_ROWS, a * PAIR_CODES + (s + 1) * PAIR_ROWS)
+                nc.tensor.matmul_mx(
+                    out=z[:],
+                    lhsT=h_codes[:, h_cols].bitcast(FP8X4),
+                    lhsT_scale=h_scales[:, h_cols],
+                    rhs=g_codes[:, g_cols].bitcast(FP8X4),
+                    rhs_scale=g_scales[:, g_cols],
+                    start=(s == 0),
+                    stop=(s == PASSES - 1),
+                )
+
+            out_cols = slice(a * PAIR_ROWS, (a + 1) * PAIR_ROWS)
+            turns = work.tile([P, PAIR_ROWS], F32)
+            nc.vector.scalar_tensor_tensor(
+                out=turns[:], in0=z[:], scalar=1.0 / TURN, in1=g_bias_turns[:, out_cols],
+                op0=ALU.mult, op1=ALU.add,
+            )
+            shifted = work.tile([P, PAIR_ROWS], F32)
+            nc.scalar.activation(out=shifted[:], in_=turns[:], func=ACT.Copy, bias=ROUND, scale=1.0)
+            minus_fraction = work.tile([P, PAIR_ROWS], F32)
+            nc.vector.scalar_tensor_tensor(
+                out=minus_fraction[:], in0=shifted[:], scalar=ROUND, in1=turns[:],
+                op0=ALU.subtract, op1=ALU.subtract,
+            )
+            c = work.tile([P, PAIR_ROWS], F32)
+            nc.scalar.activation(out=c[:], in_=minus_fraction[:], func=ACT.Sin, scale=-TURN)
+            c_squared = work.tile([P, PAIR_ROWS], F32)
+            nc.scalar.activation(out=c_squared[:], in_=c[:], func=ACT.Square)
+            sign_plus_one = work.tile([P, PAIR_ROWS], F32)
+            nc.vector.tensor_scalar(
+                out=sign_plus_one[:], in0=c_squared[:],
+                scalar1=EPS * EPS, scalar2=2.0, op0=ALU.is_ge, op1=ALU.mult,
+            )
+            flipped = work.tile([P, PAIR_ROWS], F32)
+            nc.vector.scalar_tensor_tensor(
+                out=flipped[:], in0=sign_plus_one[:], scalar=1.0, in1=c[:],
+                op0=ALU.subtract, op1=ALU.mult,
+            )
+            nc.sync.dma_start(out=out[:, out_cols], in_=flipped[:])

@@ -66,16 +66,18 @@ def tile_onehiddenlayer_s_kernel(tc, x, W, b, g, g_bias, out):
         zero_column = keep.tile([P, 1], F32)
         sine_of_zero = keep.tile([P, 1], F32)
 
-        nc.vector.memset(zero_column[:], 0.0)
+        ctx.enter_context(tc.manual_schedule())
+
         nc.vector.memset(b_as_rows[:], 0.0)
         nc.vector.memset(g_bias_as_row[:], 0.0)
+        nc.vector.memset(zero_column[:], 0.0)
         nc.vector.memset(ones[:], 1.0)
         make_identity(nc, ident[:])
-        nc.scalar.dma_start(out=b_as_rows[0:PAIRS, :], in_=b.rearrange("(a q) -> a q", a=PAIRS))
-        nc.scalar.dma_start(out=g_bias_as_row[0:1, :], in_=g_bias.rearrange("(o n) -> o n", o=1))
         nc.scalar.activation(out=sine_of_zero[:], in_=zero_column[:], func=ACT.Sin)
 
         nc.sync.dma_start(out=x_rows[:], in_=x)
+        nc.sync.dma_start(out=b_as_rows[0:PAIRS, :], in_=b.rearrange("(a q) -> a q", a=PAIRS))
+        nc.sync.dma_start(out=g_bias_as_row[0:1, :], in_=g_bias.rearrange("(o n) -> o n", o=1))
         w_pairs = W.rearrange("(a p e) k -> a p (e k)", p=P, e=2)
         for a in range(PAIRS):
             nc.sync.dma_start(out=w_rows[:, a * 2 * D : (a + 1) * 2 * D], in_=w_pairs[a])
@@ -94,37 +96,15 @@ def tile_onehiddenlayer_s_kernel(tc, x, W, b, g, g_bias, out):
             else:
                 nc.scalar.copy(out=grouped_words, in_=side_by_side)
 
-        def turn_pair(rows, grouped, a, vector_takes_second):
-            row_words = rows[:].bitcast(F32)
-            grouped_words = grouped[:].bitcast(F32).rearrange(
-                "p (a s r u) -> p a s r u", a=PAIRS, s=PASSES, r=PAIR_ROWS, u=2
-            )
-            for e in range(2):
-                i = 2 * a + e
-                turn_chunk(
-                    row_words[:, i * ROW_WORDS : (i + 1) * ROW_WORDS],
-                    grouped_words[:, a, :, e * P : (e + 1) * P, :],
-                    on_vector=(vector_takes_second and e == 1),
-                )
-
-        def quantise_pair(grouped, codes, scales, a):
-            nc.vector.quantize_mx(
-                out=codes[:, a * PAIR_CODES : (a + 1) * PAIR_CODES].bitcast(FP8X4),
-                scales=scales[:, a * PAIR_CODES : (a + 1) * PAIR_CODES],
-                in_=grouped[:, a * PAIR_CODES * PACK : (a + 1) * PAIR_CODES * PACK],
-            )
-
         turn_chunk(
             x_rows[:].bitcast(F32),
             x_grouped[:].bitcast(F32).rearrange("p (s r u) -> p s r u", s=PASSES, r=BATCH, u=2),
             on_vector=True,
         )
-        nc.vector.quantize_mx(out=x_codes[:].bitcast(FP8X4), scales=x_scales[:], in_=x_grouped[:])
-
         b_turned = psum_turned.tile([P, P], F32, tag="turned")
         nc.tensor.transpose(b_turned[:], b_as_rows[:].bitcast(F32), ident[:])
         nc.vector.tensor_copy(out=b_by_partition[:], in_=b_turned[:].bitcast(BF16)[:, 0:CHUNKS])
-
+        nc.vector.quantize_mx(out=x_codes[:].bitcast(FP8X4), scales=x_scales[:], in_=x_grouped[:])
         for half in range(D // BANK):
             cols = slice(half * BANK, (half + 1) * BANK)
             spread = psum_z.tile([P, BANK], F32, tag="z")
@@ -134,23 +114,61 @@ def tile_onehiddenlayer_s_kernel(tc, x, W, b, g, g_bias, out):
                 scalar1=1.0 / TURN, scalar2=0.25, op0=ALU.mult, op1=ALU.add,
             )
 
-        for a in range(PAIRS):
-            turn_pair(w_rows, w_grouped, a, vector_takes_second=(a % 2 == 1))
-            quantise_pair(w_grouped, w_codes, w_scales, a)
+        def is_w(n):
+            return 0 <= n < PAIRS
+
+        def is_g(n):
+            return PAIRS <= n < 2 * PAIRS
+
+        def turn(n):
+            if not (is_w(n) or is_g(n)):
+                return
+            rows, grouped = (w_rows, w_grouped) if is_w(n) else (g_rows, g_grouped)
+            a = n % PAIRS
+            row_words = rows[:].bitcast(F32)
+            grouped_words = grouped[:].bitcast(F32).rearrange(
+                "p (a s r u) -> p a s r u", a=PAIRS, s=PASSES, r=PAIR_ROWS, u=2
+            )
+            for e in range(2):
+                i = 2 * a + e
+                turn_chunk(
+                    row_words[:, i * ROW_WORDS : (i + 1) * ROW_WORDS],
+                    grouped_words[:, a, :, e * P : (e + 1) * P, :],
+                    on_vector=(a % 2 == 1 and e == 1),
+                )
+
+        def quantise(n):
+            if not (is_w(n) or is_g(n)):
+                return
+            grouped, codes, scales = (
+                (w_grouped, w_codes, w_scales) if is_w(n) else (g_grouped, g_codes, g_scales)
+            )
+            a = n % PAIRS
+            nc.vector.quantize_mx(
+                out=codes[:, a * PAIR_CODES : (a + 1) * PAIR_CODES].bitcast(FP8X4),
+                scales=scales[:, a * PAIR_CODES : (a + 1) * PAIR_CODES],
+                in_=grouped[:, a * PAIR_CODES * PACK : (a + 1) * PAIR_CODES * PACK],
+            )
 
         h_by_pass = h_grouped[:].rearrange("p (s r t) -> p s r t", s=PASSES, r=BATCH, t=PACK)
-        for s2 in range(PASSES):
-            h_turned = psum_h.tile([P, PACK, BATCH], F32)
-            for t in range(PACK):
-                i = s2 * PACK + t
+        h_turned = {}
+
+        def first_product(n):
+            if not is_w(n):
+                return
+            s2 = n // 2
+            if n % 2 == 0:
+                bank = psum_h.tile([P, PACK, BATCH], F32)
+                h_turned[s2] = bank
+            for e in range(2):
+                t = 2 * (n % 2) + e
                 for s in range(PASSES):
                     w_cols = slice(
-                        (i // 2) * PAIR_CODES + s * PAIR_ROWS + (i % 2) * P,
-                        (i // 2) * PAIR_CODES + s * PAIR_ROWS + (i % 2) * P + P,
+                        n * PAIR_CODES + s * PAIR_ROWS + e * P, n * PAIR_CODES + s * PAIR_ROWS + (e + 1) * P
                     )
                     x_cols = slice(s * BATCH, (s + 1) * BATCH)
                     nc.tensor.matmul_mx(
-                        out=h_turned[:, t, :],
+                        out=h_turned[s2][:, t, :],
                         lhsT=w_codes[:, w_cols].bitcast(FP8X4),
                         lhsT_scale=w_scales[:, w_cols],
                         rhs=x_codes[:, x_cols].bitcast(FP8X4),
@@ -158,22 +176,30 @@ def tile_onehiddenlayer_s_kernel(tc, x, W, b, g, g_bias, out):
                         start=(s == 0),
                         stop=(s == PASSES - 1),
                     )
-            nc.vector.tensor_tensor(
-                out=h_by_pass[:, s2],
-                in0=h_turned[:].rearrange("p t r -> p r t"),
-                in1=b_by_partition[:, s2 * PACK : (s2 + 1) * PACK].unsqueeze(1).to_broadcast([P, BATCH, PACK]),
-                op=ALU.add,
-            )
-            nc.vector.quantize_mx(
-                out=h_codes[:, s2 * BATCH : (s2 + 1) * BATCH].bitcast(FP8X4),
-                scales=h_scales[:, s2 * BATCH : (s2 + 1) * BATCH],
-                in_=h_grouped[:, s2 * BATCH * PACK : (s2 + 1) * BATCH * PACK],
-            )
+            if n % 2 == 1:
+                nc.vector.tensor_tensor(
+                    out=h_by_pass[:, s2],
+                    in0=h_turned[s2][:].rearrange("p t r -> p r t"),
+                    in1=b_by_partition[:, s2 * PACK : (s2 + 1) * PACK]
+                    .unsqueeze(1)
+                    .to_broadcast([P, BATCH, PACK]),
+                    op=ALU.add,
+                )
+                nc.vector.quantize_mx(
+                    out=h_codes[:, s2 * BATCH : (s2 + 1) * BATCH].bitcast(FP8X4),
+                    scales=h_scales[:, s2 * BATCH : (s2 + 1) * BATCH],
+                    in_=h_grouped[:, s2 * BATCH * PACK : (s2 + 1) * BATCH * PACK],
+                )
 
-        for a in range(PAIRS):
-            turn_pair(g_rows, g_grouped, a, vector_takes_second=False)
-            quantise_pair(g_grouped, g_codes, g_scales, a)
+        turns = {}
+        shifted = {}
+        cosine = {}
+        cosine_squared = {}
 
+        def second_product(n):
+            if not is_g(n):
+                return
+            a = n - PAIRS
             z = psum_z.tile([P, PAIR_ROWS], F32, tag="z")
             for s in range(PASSES):
                 h_cols = slice(s * BATCH, (s + 1) * BATCH)
@@ -187,32 +213,52 @@ def tile_onehiddenlayer_s_kernel(tc, x, W, b, g, g_bias, out):
                     start=(s == 0),
                     stop=(s == PASSES - 1),
                 )
-
-            out_cols = slice(a * PAIR_ROWS, (a + 1) * PAIR_ROWS)
-            turns = work.tile([P, PAIR_ROWS], F32)
+            angle = work.tile([P, PAIR_ROWS], F32)
             nc.vector.scalar_tensor_tensor(
-                out=turns[:], in0=z[:], scalar=1.0 / TURN, in1=g_bias_turns[:, out_cols],
+                out=angle[:], in0=z[:], scalar=1.0 / TURN,
+                in1=g_bias_turns[:, a * PAIR_ROWS : (a + 1) * PAIR_ROWS],
                 op0=ALU.mult, op1=ALU.add,
             )
-            shifted = work.tile([P, PAIR_ROWS], F32)
-            nc.scalar.activation(out=shifted[:], in_=turns[:], func=ACT.Copy, bias=ROUND, scale=1.0)
+            whole = work.tile([P, PAIR_ROWS], F32)
+            nc.scalar.activation(out=whole[:], in_=angle[:], func=ACT.Copy, bias=ROUND, scale=1.0)
+            turns[n] = angle
+            shifted[n] = whole
+
+        def sine(n):
+            if not is_g(n):
+                return
             minus_fraction = work.tile([P, PAIR_ROWS], F32)
             nc.vector.scalar_tensor_tensor(
-                out=minus_fraction[:], in0=shifted[:], scalar=ROUND, in1=turns[:],
+                out=minus_fraction[:], in0=shifted[n][:], scalar=ROUND, in1=turns[n][:],
                 op0=ALU.subtract, op1=ALU.subtract,
             )
             c = work.tile([P, PAIR_ROWS], F32)
             nc.scalar.activation(out=c[:], in_=minus_fraction[:], func=ACT.Sin, scale=-TURN)
             c_squared = work.tile([P, PAIR_ROWS], F32)
             nc.scalar.activation(out=c_squared[:], in_=c[:], func=ACT.Square)
+            cosine[n] = c
+            cosine_squared[n] = c_squared
+
+        def flip(n):
+            if not is_g(n):
+                return
+            a = n - PAIRS
             sign_plus_one = work.tile([P, PAIR_ROWS], F32)
             nc.vector.tensor_scalar(
-                out=sign_plus_one[:], in0=c_squared[:],
+                out=sign_plus_one[:], in0=cosine_squared[n][:],
                 scalar1=EPS * EPS, scalar2=2.0, op0=ALU.is_ge, op1=ALU.mult,
             )
             flipped = work.tile([P, PAIR_ROWS], F32)
             nc.vector.scalar_tensor_tensor(
-                out=flipped[:], in0=sign_plus_one[:], scalar=1.0, in1=c[:],
+                out=flipped[:], in0=sign_plus_one[:], scalar=1.0, in1=cosine[n][:],
                 op0=ALU.subtract, op1=ALU.mult,
             )
-            nc.sync.dma_start(out=out[:, out_cols], in_=flipped[:])
+            nc.sync.dma_start(out=out[:, a * PAIR_ROWS : (a + 1) * PAIR_ROWS], in_=flipped[:])
+
+        for step in range(2 * PAIRS + 4):
+            flip(step - 4)
+            sine(step - 3)
+            first_product(step - 2)
+            second_product(step - 2)
+            quantise(step - 1)
+            turn(step)

@@ -134,7 +134,7 @@ def tile_onehiddenlayer_s_kernel(tc, x, W, b, g, g_bias, out):
                 turn_chunk(
                     row_words[:, i * ROW_WORDS : (i + 1) * ROW_WORDS],
                     grouped_words[:, a, :, e * P : (e + 1) * P, :],
-                    on_vector=(a % 2 == 1 and e == 1),
+                    on_vector=False,
                 )
 
         def quantise(n):
@@ -151,24 +151,21 @@ def tile_onehiddenlayer_s_kernel(tc, x, W, b, g, g_bias, out):
             )
 
         h_by_pass = h_grouped[:].rearrange("p (s r t) -> p s r t", s=PASSES, r=BATCH, t=PACK)
-        h_turned = {}
 
         def first_product(n):
-            if not is_w(n):
+            if not (is_w(n) and n % 2 == 1):
                 return
             s2 = n // 2
-            if n % 2 == 0:
-                bank = psum_h.tile([P, PACK, BATCH], F32)
-                h_turned[s2] = bank
-            for e in range(2):
-                t = 2 * (n % 2) + e
+            h_turned = psum_h.tile([P, PACK, BATCH], F32)
+            for t in range(PACK):
+                a, e = 2 * s2 + t // 2, t % 2
                 for s in range(PASSES):
                     w_cols = slice(
-                        n * PAIR_CODES + s * PAIR_ROWS + e * P, n * PAIR_CODES + s * PAIR_ROWS + (e + 1) * P
+                        a * PAIR_CODES + s * PAIR_ROWS + e * P, a * PAIR_CODES + s * PAIR_ROWS + (e + 1) * P
                     )
                     x_cols = slice(s * BATCH, (s + 1) * BATCH)
                     nc.tensor.matmul_mx(
-                        out=h_turned[s2][:, t, :],
+                        out=h_turned[:, t, :],
                         lhsT=w_codes[:, w_cols].bitcast(FP8X4),
                         lhsT_scale=w_scales[:, w_cols],
                         rhs=x_codes[:, x_cols].bitcast(FP8X4),
@@ -176,25 +173,25 @@ def tile_onehiddenlayer_s_kernel(tc, x, W, b, g, g_bias, out):
                         start=(s == 0),
                         stop=(s == PASSES - 1),
                     )
-            if n % 2 == 1:
-                nc.vector.tensor_tensor(
-                    out=h_by_pass[:, s2],
-                    in0=h_turned[s2][:].rearrange("p t r -> p r t"),
-                    in1=b_by_partition[:, s2 * PACK : (s2 + 1) * PACK]
-                    .unsqueeze(1)
-                    .to_broadcast([P, BATCH, PACK]),
-                    op=ALU.add,
-                )
-                nc.vector.quantize_mx(
-                    out=h_codes[:, s2 * BATCH : (s2 + 1) * BATCH].bitcast(FP8X4),
-                    scales=h_scales[:, s2 * BATCH : (s2 + 1) * BATCH],
-                    in_=h_grouped[:, s2 * BATCH * PACK : (s2 + 1) * BATCH * PACK],
-                )
+            nc.vector.tensor_tensor(
+                out=h_by_pass[:, s2],
+                in0=h_turned[:].rearrange("p t r -> p r t"),
+                in1=b_by_partition[:, s2 * PACK : (s2 + 1) * PACK]
+                .unsqueeze(1)
+                .to_broadcast([P, BATCH, PACK]),
+                op=ALU.add,
+            )
+            nc.vector.quantize_mx(
+                out=h_codes[:, s2 * BATCH : (s2 + 1) * BATCH].bitcast(FP8X4),
+                scales=h_scales[:, s2 * BATCH : (s2 + 1) * BATCH],
+                in_=h_grouped[:, s2 * BATCH * PACK : (s2 + 1) * BATCH * PACK],
+            )
 
         turns = {}
         shifted = {}
         cosine = {}
-        cosine_squared = {}
+        cosine_size = {}
+        sign_plus_one = {}
 
         def second_product(n):
             if not is_g(n):
@@ -234,31 +231,36 @@ def tile_onehiddenlayer_s_kernel(tc, x, W, b, g, g_bias, out):
             )
             c = work.tile([P, PAIR_ROWS], F32)
             nc.scalar.activation(out=c[:], in_=minus_fraction[:], func=ACT.Sin, scale=-TURN)
-            c_squared = work.tile([P, PAIR_ROWS], F32)
-            nc.scalar.activation(out=c_squared[:], in_=c[:], func=ACT.Square)
+            c_size = work.tile([P, PAIR_ROWS], F32)
+            nc.scalar.activation(out=c_size[:], in_=c[:], func=ACT.Abs)
             cosine[n] = c
-            cosine_squared[n] = c_squared
+            cosine_size[n] = c_size
+
+        def compare(n):
+            if not is_g(n):
+                return
+            stays = work.tile([P, PAIR_ROWS], F32)
+            nc.vector.tensor_scalar(
+                out=stays[:], in0=cosine_size[n][:], scalar1=EPS, scalar2=2.0, op0=ALU.is_ge, op1=ALU.mult
+            )
+            sign_plus_one[n] = stays
 
         def flip(n):
             if not is_g(n):
                 return
             a = n - PAIRS
-            sign_plus_one = work.tile([P, PAIR_ROWS], F32)
-            nc.vector.tensor_scalar(
-                out=sign_plus_one[:], in0=cosine_squared[n][:],
-                scalar1=EPS * EPS, scalar2=2.0, op0=ALU.is_ge, op1=ALU.mult,
-            )
             flipped = work.tile([P, PAIR_ROWS], F32)
             nc.vector.scalar_tensor_tensor(
-                out=flipped[:], in0=sign_plus_one[:], scalar=1.0, in1=cosine[n][:],
+                out=flipped[:], in0=sign_plus_one[n][:], scalar=1.0, in1=cosine[n][:],
                 op0=ALU.subtract, op1=ALU.mult,
             )
             nc.sync.dma_start(out=out[:, a * PAIR_ROWS : (a + 1) * PAIR_ROWS], in_=flipped[:])
 
-        for step in range(2 * PAIRS + 4):
-            flip(step - 4)
-            sine(step - 3)
-            first_product(step - 2)
-            second_product(step - 2)
-            quantise(step - 1)
+        for step in range(2 * PAIRS + 6):
             turn(step)
+            quantise(step - 1)
+            first_product(step - 2)
+            second_product(step - 3)
+            sine(step - 4)
+            compare(step - 5)
+            flip(step - 6)

@@ -19,10 +19,9 @@ BATCH = 128
 D = 1024
 PASSES = D // K_PASS
 CHUNKS = D // P
-PAIRS = CHUNKS // 2
-PAIR_ROWS = 2 * P
 ROW_WORDS = D // 2
-PAIR_CODES = PASSES * PAIR_ROWS
+CHUNK_CODES = PASSES * P
+PAIR = 2 * P
 BANK = 512
 
 EPS = 0.01
@@ -36,7 +35,7 @@ def tile_onehiddenlayer_s_kernel(tc, x, W, b, g, g_bias, out):
     nc = tc.nc
     with ExitStack() as ctx:
         keep = ctx.enter_context(tc.tile_pool(name="keep", bufs=1))
-        work = ctx.enter_context(tc.tile_pool(name="work", bufs=PAIRS))
+        work = ctx.enter_context(tc.tile_pool(name="work", bufs=D // PAIR))
         psum_turned = ctx.enter_context(tc.psum_pool(name="psum_turned", bufs=4))
         psum_h = ctx.enter_context(tc.psum_pool(name="psum_h", bufs=PASSES))
         psum_z = ctx.enter_context(tc.psum_pool(name="psum_z", bufs=2))
@@ -48,18 +47,18 @@ def tile_onehiddenlayer_s_kernel(tc, x, W, b, g, g_bias, out):
         w_grouped = keep.tile([P, CHUNKS * D], BF16, align_bytes=64)
         g_grouped = keep.tile([P, CHUNKS * D], BF16, align_bytes=64)
         h_grouped = keep.tile([P, D], BF16, align_bytes=64)
-        x_codes = keep.tile([P, PASSES * BATCH], U32, align_bytes=64)
-        x_scales = keep.tile([P, PASSES * BATCH], U8, align_bytes=64)
-        w_codes = keep.tile([P, PAIRS * PAIR_CODES], U32, align_bytes=64)
-        w_scales = keep.tile([P, PAIRS * PAIR_CODES], U8, align_bytes=64)
-        g_codes = keep.tile([P, PAIRS * PAIR_CODES], U32, align_bytes=64)
-        g_scales = keep.tile([P, PAIRS * PAIR_CODES], U8, align_bytes=64)
-        h_codes = keep.tile([P, PASSES * BATCH], U32, align_bytes=64)
-        h_scales = keep.tile([P, PASSES * BATCH], U8, align_bytes=64)
+        x_codes = keep.tile([P, CHUNK_CODES], U32, align_bytes=64)
+        x_scales = keep.tile([P, CHUNK_CODES], U8, align_bytes=64)
+        w_codes = keep.tile([P, CHUNKS * CHUNK_CODES], U32, align_bytes=64)
+        w_scales = keep.tile([P, CHUNKS * CHUNK_CODES], U8, align_bytes=64)
+        g_codes = keep.tile([P, CHUNKS * CHUNK_CODES], U32, align_bytes=64)
+        g_scales = keep.tile([P, CHUNKS * CHUNK_CODES], U8, align_bytes=64)
+        h_codes = keep.tile([P, CHUNK_CODES], U32, align_bytes=64)
+        h_scales = keep.tile([P, CHUNK_CODES], U8, align_bytes=64)
 
         ident = keep.tile([P, P], F32)
         ones = keep.tile([P, P], BF16)
-        b_as_rows = keep.tile([P, PAIR_ROWS], BF16)
+        b_as_rows = keep.tile([P, 2 * P], BF16)
         g_bias_as_row = keep.tile([P, D], BF16)
         b_by_partition = keep.tile([P, CHUNKS], F32)
         g_bias_turns = keep.tile([P, D], F32)
@@ -76,35 +75,55 @@ def tile_onehiddenlayer_s_kernel(tc, x, W, b, g, g_bias, out):
         nc.scalar.activation(out=sine_of_zero[:], in_=zero_column[:], func=ACT.Sin)
 
         nc.sync.dma_start(out=x_rows[:], in_=x)
-        nc.sync.dma_start(out=b_as_rows[0:PAIRS, :], in_=b.rearrange("(a q) -> a q", a=PAIRS))
+        nc.sync.dma_start(out=b_as_rows[0 : CHUNKS // 2, :], in_=b.rearrange("(a q) -> a q", q=2 * P))
         nc.sync.dma_start(out=g_bias_as_row[0:1, :], in_=g_bias.rearrange("(o n) -> o n", o=1))
         w_pairs = W.rearrange("(a p e) k -> a p (e k)", p=P, e=2)
-        for a in range(PAIRS):
+        for a in range(CHUNKS // 2):
             nc.sync.dma_start(out=w_rows[:, a * 2 * D : (a + 1) * 2 * D], in_=w_pairs[a])
         for i in range(CHUNKS):
             nc.sync.dma_start(out=g_rows[:, i * D : (i + 1) * D], in_=g[i * P : (i + 1) * P, :])
 
-        def turn_chunk(row_words, grouped_words, on_vector):
+        def turn_chunk(rows, grouped, i, on_vector):
+            row_words = rows[:].bitcast(F32)[:, i * ROW_WORDS : (i + 1) * ROW_WORDS]
+            grouped_words = grouped[:].bitcast(F32)[:, i * ROW_WORDS : (i + 1) * ROW_WORDS]
             turned = psum_turned.tile([P, PASSES, 2, P], F32)
             for s in range(PASSES):
                 for u in range(2):
                     first = (2 * s + u) * P
                     nc.tensor.transpose(turned[:, s, u, :], row_words[:, first : first + P], ident[:])
             side_by_side = turned[:].rearrange("p s u r -> p s r u")
+            contiguous = grouped_words.rearrange("p (s r u) -> p s r u", s=PASSES, r=P, u=2)
             if on_vector:
-                nc.vector.tensor_copy(out=grouped_words, in_=side_by_side)
+                nc.vector.tensor_copy(out=contiguous, in_=side_by_side)
             else:
-                nc.scalar.copy(out=grouped_words, in_=side_by_side)
+                nc.scalar.copy(out=contiguous, in_=side_by_side)
 
-        turn_chunk(
-            x_rows[:].bitcast(F32),
-            x_grouped[:].bitcast(F32).rearrange("p (s r u) -> p s r u", s=PASSES, r=BATCH, u=2),
-            on_vector=True,
-        )
+        def quantise_chunk(grouped, codes, scales, i):
+            nc.vector.quantize_mx(
+                out=codes[:, i * CHUNK_CODES : (i + 1) * CHUNK_CODES].bitcast(FP8X4),
+                scales=scales[:, i * CHUNK_CODES : (i + 1) * CHUNK_CODES],
+                in_=grouped[:, i * D : (i + 1) * D],
+            )
+
+        def multiply(acc, left_codes, left_scales, left_chunk, right_codes, right_scales, right_chunk):
+            for s in range(PASSES):
+                left = slice(left_chunk * CHUNK_CODES + s * P, left_chunk * CHUNK_CODES + (s + 1) * P)
+                right = slice(right_chunk * CHUNK_CODES + s * P, right_chunk * CHUNK_CODES + (s + 1) * P)
+                nc.tensor.matmul_mx(
+                    out=acc,
+                    lhsT=left_codes[:, left].bitcast(FP8X4),
+                    lhsT_scale=left_scales[:, left],
+                    rhs=right_codes[:, right].bitcast(FP8X4),
+                    rhs_scale=right_scales[:, right],
+                    start=(s == 0),
+                    stop=(s == PASSES - 1),
+                )
+
+        turn_chunk(x_rows, x_grouped, 0, on_vector=True)
         b_turned = psum_turned.tile([P, P], F32, tag="turned")
         nc.tensor.transpose(b_turned[:], b_as_rows[:].bitcast(F32), ident[:])
         nc.vector.tensor_copy(out=b_by_partition[:], in_=b_turned[:].bitcast(BF16)[:, 0:CHUNKS])
-        nc.vector.quantize_mx(out=x_codes[:].bitcast(FP8X4), scales=x_scales[:], in_=x_grouped[:])
+        quantise_chunk(x_grouped, x_codes, x_scales, 0)
         for half in range(D // BANK):
             cols = slice(half * BANK, (half + 1) * BANK)
             spread = psum_z.tile([P, BANK], F32, tag="z")
@@ -115,77 +134,48 @@ def tile_onehiddenlayer_s_kernel(tc, x, W, b, g, g_bias, out):
             )
 
         def is_w(n):
-            return 0 <= n < PAIRS
+            return 0 <= n < CHUNKS
 
         def is_g(n):
-            return PAIRS <= n < 2 * PAIRS
+            return CHUNKS <= n < 2 * CHUNKS
 
         def turn(n):
-            if not (is_w(n) or is_g(n)):
-                return
-            rows, grouped = (w_rows, w_grouped) if is_w(n) else (g_rows, g_grouped)
-            a = n % PAIRS
-            row_words = rows[:].bitcast(F32)
-            grouped_words = grouped[:].bitcast(F32).rearrange(
-                "p (a s r u) -> p a s r u", a=PAIRS, s=PASSES, r=PAIR_ROWS, u=2
-            )
-            for e in range(2):
-                i = 2 * a + e
-                turn_chunk(
-                    row_words[:, i * ROW_WORDS : (i + 1) * ROW_WORDS],
-                    grouped_words[:, a, :, e * P : (e + 1) * P, :],
-                    on_vector=False,
-                )
+            if is_w(n):
+                turn_chunk(w_rows, w_grouped, n, on_vector=False)
+            if is_g(n):
+                turn_chunk(g_rows, g_grouped, n - CHUNKS, on_vector=False)
 
         def quantise(n):
-            if not (is_w(n) or is_g(n)):
-                return
-            grouped, codes, scales = (
-                (w_grouped, w_codes, w_scales) if is_w(n) else (g_grouped, g_codes, g_scales)
-            )
-            a = n % PAIRS
-            nc.vector.quantize_mx(
-                out=codes[:, a * PAIR_CODES : (a + 1) * PAIR_CODES].bitcast(FP8X4),
-                scales=scales[:, a * PAIR_CODES : (a + 1) * PAIR_CODES],
-                in_=grouped[:, a * PAIR_CODES * PACK : (a + 1) * PAIR_CODES * PACK],
-            )
+            if is_w(n):
+                quantise_chunk(w_grouped, w_codes, w_scales, n)
+            if is_g(n):
+                quantise_chunk(g_grouped, g_codes, g_scales, n - CHUNKS)
 
-        h_by_pass = h_grouped[:].rearrange("p (s r t) -> p s r t", s=PASSES, r=BATCH, t=PACK)
+        h_turned = {}
 
         def first_product(n):
             if not (is_w(n) and n % 2 == 1):
                 return
-            s2 = n // 2
-            h_turned = psum_h.tile([P, PACK, BATCH], F32)
-            for t in range(PACK):
-                a, e = 2 * s2 + t // 2, t % 2
-                for s in range(PASSES):
-                    w_cols = slice(
-                        a * PAIR_CODES + s * PAIR_ROWS + e * P, a * PAIR_CODES + s * PAIR_ROWS + (e + 1) * P
-                    )
-                    x_cols = slice(s * BATCH, (s + 1) * BATCH)
-                    nc.tensor.matmul_mx(
-                        out=h_turned[:, t, :],
-                        lhsT=w_codes[:, w_cols].bitcast(FP8X4),
-                        lhsT_scale=w_scales[:, w_cols],
-                        rhs=x_codes[:, x_cols].bitcast(FP8X4),
-                        rhs_scale=x_scales[:, x_cols],
-                        start=(s == 0),
-                        stop=(s == PASSES - 1),
-                    )
-            nc.vector.tensor_tensor(
-                out=h_by_pass[:, s2],
-                in0=h_turned[:].rearrange("p t r -> p r t"),
-                in1=b_by_partition[:, s2 * PACK : (s2 + 1) * PACK]
-                .unsqueeze(1)
-                .to_broadcast([P, BATCH, PACK]),
-                op=ALU.add,
-            )
-            nc.vector.quantize_mx(
-                out=h_codes[:, s2 * BATCH : (s2 + 1) * BATCH].bitcast(FP8X4),
-                scales=h_scales[:, s2 * BATCH : (s2 + 1) * BATCH],
-                in_=h_grouped[:, s2 * BATCH * PACK : (s2 + 1) * BATCH * PACK],
-            )
+            s2 = n // PACK
+            if n % PACK == 1:
+                bank = psum_h.tile([P, PACK, BATCH], F32)
+                h_turned[s2] = bank
+            for i in (n - 1, n):
+                multiply(h_turned[s2][:, i % PACK, :], w_codes, w_scales, i, x_codes, x_scales, 0)
+            if n % PACK == PACK - 1:
+                nc.vector.tensor_tensor(
+                    out=h_grouped[:, s2 * K_PASS : (s2 + 1) * K_PASS].rearrange("p (r t) -> p r t", t=PACK),
+                    in0=h_turned[s2][:].rearrange("p t r -> p r t"),
+                    in1=b_by_partition[:, s2 * PACK : (s2 + 1) * PACK]
+                    .unsqueeze(1)
+                    .to_broadcast([P, BATCH, PACK]),
+                    op=ALU.add,
+                )
+                nc.vector.quantize_mx(
+                    out=h_codes[:, s2 * BATCH : (s2 + 1) * BATCH].bitcast(FP8X4),
+                    scales=h_scales[:, s2 * BATCH : (s2 + 1) * BATCH],
+                    in_=h_grouped[:, s2 * K_PASS : (s2 + 1) * K_PASS],
+                )
 
         turns = {}
         shifted = {}
@@ -194,73 +184,63 @@ def tile_onehiddenlayer_s_kernel(tc, x, W, b, g, g_bias, out):
         sign_plus_one = {}
 
         def second_product(n):
-            if not is_g(n):
+            if not (is_g(n) and n % 2 == 1):
                 return
-            a = n - PAIRS
-            z = psum_z.tile([P, PAIR_ROWS], F32, tag="z")
-            for s in range(PASSES):
-                h_cols = slice(s * BATCH, (s + 1) * BATCH)
-                g_cols = slice(a * PAIR_CODES + s * PAIR_ROWS, a * PAIR_CODES + (s + 1) * PAIR_ROWS)
-                nc.tensor.matmul_mx(
-                    out=z[:],
-                    lhsT=h_codes[:, h_cols].bitcast(FP8X4),
-                    lhsT_scale=h_scales[:, h_cols],
-                    rhs=g_codes[:, g_cols].bitcast(FP8X4),
-                    rhs_scale=g_scales[:, g_cols],
-                    start=(s == 0),
-                    stop=(s == PASSES - 1),
-                )
-            angle = work.tile([P, PAIR_ROWS], F32)
+            z = psum_z.tile([P, PAIR], F32, tag="z")
+            for e in range(2):
+                multiply(z[:, e * P : (e + 1) * P], h_codes, h_scales, 0, g_codes, g_scales, n - CHUNKS - 1 + e)
+            first_column = (n - CHUNKS - 1) * P
+            angle = work.tile([P, PAIR], F32)
             nc.vector.scalar_tensor_tensor(
                 out=angle[:], in0=z[:], scalar=1.0 / TURN,
-                in1=g_bias_turns[:, a * PAIR_ROWS : (a + 1) * PAIR_ROWS],
+                in1=g_bias_turns[:, first_column : first_column + PAIR],
                 op0=ALU.mult, op1=ALU.add,
             )
-            whole = work.tile([P, PAIR_ROWS], F32)
+            whole = work.tile([P, PAIR], F32)
             nc.scalar.activation(out=whole[:], in_=angle[:], func=ACT.Copy, bias=ROUND, scale=1.0)
             turns[n] = angle
             shifted[n] = whole
 
         def sine(n):
-            if not is_g(n):
+            if n not in turns:
                 return
-            minus_fraction = work.tile([P, PAIR_ROWS], F32)
+            minus_fraction = work.tile([P, PAIR], F32)
             nc.vector.scalar_tensor_tensor(
                 out=minus_fraction[:], in0=shifted[n][:], scalar=ROUND, in1=turns[n][:],
                 op0=ALU.subtract, op1=ALU.subtract,
             )
-            c = work.tile([P, PAIR_ROWS], F32)
+            c = work.tile([P, PAIR], F32)
             nc.scalar.activation(out=c[:], in_=minus_fraction[:], func=ACT.Sin, scale=-TURN)
-            c_size = work.tile([P, PAIR_ROWS], F32)
+            c_size = work.tile([P, PAIR], F32)
             nc.scalar.activation(out=c_size[:], in_=c[:], func=ACT.Abs)
             cosine[n] = c
             cosine_size[n] = c_size
 
         def compare(n):
-            if not is_g(n):
+            if n not in cosine:
                 return
-            stays = work.tile([P, PAIR_ROWS], F32)
+            stays = work.tile([P, PAIR], F32)
             nc.vector.tensor_scalar(
                 out=stays[:], in0=cosine_size[n][:], scalar1=EPS, scalar2=2.0, op0=ALU.is_ge, op1=ALU.mult
             )
             sign_plus_one[n] = stays
 
         def flip(n):
-            if not is_g(n):
+            if n not in sign_plus_one:
                 return
-            a = n - PAIRS
-            flipped = work.tile([P, PAIR_ROWS], F32)
+            first_column = (n - CHUNKS - 1) * P
+            flipped = work.tile([P, PAIR], F32)
             nc.vector.scalar_tensor_tensor(
                 out=flipped[:], in0=sign_plus_one[n][:], scalar=1.0, in1=cosine[n][:],
                 op0=ALU.subtract, op1=ALU.mult,
             )
-            nc.sync.dma_start(out=out[:, a * PAIR_ROWS : (a + 1) * PAIR_ROWS], in_=flipped[:])
+            nc.sync.dma_start(out=out[:, first_column : first_column + PAIR], in_=flipped[:])
 
-        for step in range(2 * PAIRS + 6):
+        for step in range(2 * CHUNKS + 11):
             turn(step)
-            quantise(step - 1)
-            first_product(step - 2)
-            second_product(step - 3)
-            sine(step - 4)
-            compare(step - 5)
-            flip(step - 6)
+            quantise(step - 2)
+            first_product(step - 4)
+            second_product(step - 5)
+            sine(step - 7)
+            compare(step - 9)
+            flip(step - 11)

@@ -23,6 +23,12 @@ ROW_WORDS = D // 2
 CHUNK_CODES = PASSES * P
 PAIR = 2 * P
 BANK = 512
+PSUM_BANKS = 8
+
+QUANTISE_LAG = 2
+FIRST_PRODUCT_LAG = 5
+SECOND_PRODUCT_LAG = 7
+PAIR_STEPS = 2
 
 EPS = 0.01
 TURN = 2.0 * math.pi
@@ -36,7 +42,7 @@ def tile_onehiddenlayer_s_kernel(tc, x, W, b, g, g_bias, out):
     with ExitStack() as ctx:
         keep = ctx.enter_context(tc.tile_pool(name="keep", bufs=1))
         work = ctx.enter_context(tc.tile_pool(name="work", bufs=D // PAIR))
-        psum_turned = ctx.enter_context(tc.psum_pool(name="psum_turned", bufs=4))
+        psum_turned = ctx.enter_context(tc.psum_pool(name="psum_turned", bufs=PSUM_BANKS - PASSES - 2))
         psum_h = ctx.enter_context(tc.psum_pool(name="psum_h", bufs=PASSES))
         psum_z = ctx.enter_context(tc.psum_pool(name="psum_z", bufs=2))
 
@@ -75,11 +81,11 @@ def tile_onehiddenlayer_s_kernel(tc, x, W, b, g, g_bias, out):
         nc.scalar.activation(out=sine_of_zero[:], in_=zero_column[:], func=ACT.Sin)
 
         nc.sync.dma_start(out=x_rows[:], in_=x)
-        nc.sync.dma_start(out=b_as_rows[0 : CHUNKS // 2, :], in_=b.rearrange("(a q) -> a q", q=2 * P))
+        nc.sync.dma_start(out=b_as_rows[0 : CHUNKS // 2, :], in_=b.rearrange("(a c) -> a c", c=2 * P))
         nc.sync.dma_start(out=g_bias_as_row[0:1, :], in_=g_bias.rearrange("(o n) -> o n", o=1))
-        w_pairs = W.rearrange("(a p e) k -> a p (e k)", p=P, e=2)
-        for a in range(CHUNKS // 2):
-            nc.sync.dma_start(out=w_rows[:, a * 2 * D : (a + 1) * 2 * D], in_=w_pairs[a])
+        w_chunks = W.rearrange("(a p e) k -> a e p k", p=P, e=2)
+        for i in range(CHUNKS):
+            nc.sync.dma_start(out=w_rows[:, i * D : (i + 1) * D], in_=w_chunks[i // 2, i % 2])
         for i in range(CHUNKS):
             nc.sync.dma_start(out=g_rows[:, i * D : (i + 1) * D], in_=g[i * P : (i + 1) * P, :])
 
@@ -179,6 +185,7 @@ def tile_onehiddenlayer_s_kernel(tc, x, W, b, g, g_bias, out):
 
         turns = {}
         shifted = {}
+        fraction = {}
         cosine = {}
         cosine_size = {}
         sign_plus_one = {}
@@ -196,28 +203,41 @@ def tile_onehiddenlayer_s_kernel(tc, x, W, b, g, g_bias, out):
                 in1=g_bias_turns[:, first_column : first_column + PAIR],
                 op0=ALU.mult, op1=ALU.add,
             )
-            whole = work.tile([P, PAIR], F32)
-            nc.scalar.activation(out=whole[:], in_=angle[:], func=ACT.Copy, bias=ROUND, scale=1.0)
             turns[n] = angle
+
+        def shift(n):
+            if n not in turns:
+                return
+            whole = work.tile([P, PAIR], F32)
+            nc.scalar.activation(out=whole[:], in_=turns[n][:], func=ACT.Copy, bias=ROUND, scale=1.0)
             shifted[n] = whole
 
-        def sine(n):
-            if n not in turns:
+        def take_off_whole_turns(n):
+            if n not in shifted:
                 return
             minus_fraction = work.tile([P, PAIR], F32)
             nc.vector.scalar_tensor_tensor(
                 out=minus_fraction[:], in0=shifted[n][:], scalar=ROUND, in1=turns[n][:],
                 op0=ALU.subtract, op1=ALU.subtract,
             )
+            fraction[n] = minus_fraction
+
+        def sine(n):
+            if n not in fraction:
+                return
             c = work.tile([P, PAIR], F32)
-            nc.scalar.activation(out=c[:], in_=minus_fraction[:], func=ACT.Sin, scale=-TURN)
-            c_size = work.tile([P, PAIR], F32)
-            nc.scalar.activation(out=c_size[:], in_=c[:], func=ACT.Abs)
+            nc.scalar.activation(out=c[:], in_=fraction[n][:], func=ACT.Sin, scale=-TURN)
             cosine[n] = c
+
+        def size(n):
+            if n not in cosine:
+                return
+            c_size = work.tile([P, PAIR], F32)
+            nc.scalar.activation(out=c_size[:], in_=cosine[n][:], func=ACT.Abs)
             cosine_size[n] = c_size
 
         def compare(n):
-            if n not in cosine:
+            if n not in cosine_size:
                 return
             stays = work.tile([P, PAIR], F32)
             nc.vector.tensor_scalar(
@@ -236,11 +256,10 @@ def tile_onehiddenlayer_s_kernel(tc, x, W, b, g, g_bias, out):
             )
             nc.sync.dma_start(out=out[:, first_column : first_column + PAIR], in_=flipped[:])
 
-        for step in range(2 * CHUNKS + 11):
+        pair_stages = (second_product, shift, take_off_whole_turns, sine, size, compare, flip)
+        for step in range(2 * CHUNKS + SECOND_PRODUCT_LAG + PAIR_STEPS * (len(pair_stages) - 1)):
             turn(step)
-            quantise(step - 2)
-            first_product(step - 4)
-            second_product(step - 5)
-            sine(step - 7)
-            compare(step - 9)
-            flip(step - 11)
+            quantise(step - QUANTISE_LAG)
+            first_product(step - FIRST_PRODUCT_LAG)
+            for depth, stage in enumerate(pair_stages):
+                stage(step - SECOND_PRODUCT_LAG - PAIR_STEPS * depth)

import math
from contextlib import ExitStack

import concourse.mybir as mybir
from concourse.masks import make_identity

F32 = mybir.dt.float32
BF16 = mybir.dt.bfloat16
U32 = mybir.dt.uint32
U8 = mybir.dt.uint8
FP8X4 = mybir.dt.float8_e4m3fn_x4
ALU = mybir.AluOpType
ACT = mybir.ActivationFunctionType

P = 128
PACK = 4
K_PASS = P * PACK
BATCH = 128
D = 1024
PASSES = D // K_PASS
CHUNKS = D // P
ROW_WORDS = D // 2
CHUNK_CODES = PASSES * P
PAIR = 2 * P
BANK = 512
PSUM_BANKS = 8

QUANTISE_LAG = 2
FIRST_PRODUCT_LAG = 5
SECOND_PRODUCT_LAG = 7
PAIR_STEPS = 2

EPS = 0.01
TURN = 2.0 * math.pi
ROUND = 1.5 * 2.0**23

FLOPS = 2 * 2 * BATCH * D * D


def tile_onehiddenlayer_s_kernel(tc, x, W, b, g, g_bias, out):
    nc = tc.nc
    with ExitStack() as ctx:
        keep = ctx.enter_context(tc.tile_pool(name="keep", bufs=1))
        work = ctx.enter_context(tc.tile_pool(name="work", bufs=D // PAIR))
        psum_turned = ctx.enter_context(tc.psum_pool(name="psum_turned", bufs=PSUM_BANKS - PASSES - 2))
        psum_h = ctx.enter_context(tc.psum_pool(name="psum_h", bufs=PASSES))
        psum_z = ctx.enter_context(tc.psum_pool(name="psum_z", bufs=2))

        x_rows = keep.tile([P, D], BF16)
        w_rows = keep.tile([P, CHUNKS * D], BF16)
        g_rows = keep.tile([P, CHUNKS * D], BF16)
        x_grouped = keep.tile([P, D], BF16, align_bytes=64)
        w_grouped = keep.tile([P, CHUNKS * D], BF16, align_bytes=64)
        g_grouped = keep.tile([P, CHUNKS * D], BF16, align_bytes=64)
        h_grouped = keep.tile([P, D], BF16, align_bytes=64)
        x_codes = keep.tile([P, CHUNK_CODES], U32, align_bytes=64)
        x_scales = keep.tile([P, CHUNK_CODES], U8, align_bytes=64)
        w_codes = keep.tile([P, CHUNKS * CHUNK_CODES], U32, align_bytes=64)
        w_scales = keep.tile([P, CHUNKS * CHUNK_CODES], U8, align_bytes=64)
        g_codes = keep.tile([P, CHUNKS * CHUNK_CODES], U32, align_bytes=64)
        g_scales = keep.tile([P, CHUNKS * CHUNK_CODES], U8, align_bytes=64)
        h_codes = keep.tile([P, CHUNK_CODES], U32, align_bytes=64)
        h_scales = keep.tile([P, CHUNK_CODES], U8, align_bytes=64)

        ident = keep.tile([P, P], F32)
        ones = keep.tile([P, P], BF16)
        b_as_rows = keep.tile([P, 2 * P], BF16)
        g_bias_as_row = keep.tile([P, D], BF16)
        b_by_partition = keep.tile([P, CHUNKS], F32)
        g_bias_turns = keep.tile([P, D], F32)
        zero_column = keep.tile([P, 1], F32)
        sine_of_zero = keep.tile([P, 1], F32)

        ctx.enter_context(tc.manual_schedule())

        nc.vector.memset(b_as_rows[:], 0.0)
        nc.vector.memset(g_bias_as_row[:], 0.0)
        nc.vector.memset(zero_column[:], 0.0)
        nc.vector.memset(ones[:], 1.0)
        make_identity(nc, ident[:])
        nc.scalar.activation(out=sine_of_zero[:], in_=zero_column[:], func=ACT.Sin)

        nc.sync.dma_start(out=x_rows[:], in_=x)
        nc.sync.dma_start(out=b_as_rows[0 : CHUNKS // 2, :], in_=b.rearrange("(a c) -> a c", c=2 * P))
        nc.sync.dma_start(out=g_bias_as_row[0:1, :], in_=g_bias.rearrange("(o n) -> o n", o=1))
        w_chunks = W.rearrange("(a p e) k -> a e p k", p=P, e=2)
        for i in range(CHUNKS):
            nc.sync.dma_start(out=w_rows[:, i * D : (i + 1) * D], in_=w_chunks[i // 2, i % 2])
        for i in range(CHUNKS):
            nc.sync.dma_start(out=g_rows[:, i * D : (i + 1) * D], in_=g[i * P : (i + 1) * P, :])

        def turn_chunk(rows, grouped, i, on_vector):
            row_words = rows[:].bitcast(F32)[:, i * ROW_WORDS : (i + 1) * ROW_WORDS]
            grouped_words = grouped[:].bitcast(F32)[:, i * ROW_WORDS : (i + 1) * ROW_WORDS]
            turned = psum_turned.tile([P, PASSES, 2, P], F32)
            for s in range(PASSES):
                for u in range(2):
                    first = (2 * s + u) * P
                    nc.tensor.transpose(turned[:, s, u, :], row_words[:, first : first + P], ident[:])
            side_by_side = turned[:].rearrange("p s u r -> p s r u")
            contiguous = grouped_words.rearrange("p (s r u) -> p s r u", s=PASSES, r=P, u=2)
            if on_vector:
                nc.vector.tensor_copy(out=contiguous, in_=side_by_side)
            else:
                nc.scalar.copy(out=contiguous, in_=side_by_side)

        def quantise_chunk(grouped, codes, scales, i):
            nc.vector.quantize_mx(
                out=codes[:, i * CHUNK_CODES : (i + 1) * CHUNK_CODES].bitcast(FP8X4),
                scales=scales[:, i * CHUNK_CODES : (i + 1) * CHUNK_CODES],
                in_=grouped[:, i * D : (i + 1) * D],
            )

        def multiply(acc, left_codes, left_scales, left_chunk, right_codes, right_scales, right_chunk):
            for s in range(PASSES):
                left = slice(left_chunk * CHUNK_CODES + s * P, left_chunk * CHUNK_CODES + (s + 1) * P)
                right = slice(right_chunk * CHUNK_CODES + s * P, right_chunk * CHUNK_CODES + (s + 1) * P)
                nc.tensor.matmul_mx(
                    out=acc,
                    lhsT=left_codes[:, left].bitcast(FP8X4),
                    lhsT_scale=left_scales[:, left],
                    rhs=right_codes[:, right].bitcast(FP8X4),
                    rhs_scale=right_scales[:, right],
                    start=(s == 0),
                    stop=(s == PASSES - 1),
                )

        turn_chunk(x_rows, x_grouped, 0, on_vector=True)
        b_turned = psum_turned.tile([P, P], F32, tag="turned")
        nc.tensor.transpose(b_turned[:], b_as_rows[:].bitcast(F32), ident[:])
        nc.vector.tensor_copy(out=b_by_partition[:], in_=b_turned[:].bitcast(BF16)[:, 0:CHUNKS])
        quantise_chunk(x_grouped, x_codes, x_scales, 0)
        for half in range(D // BANK):
            cols = slice(half * BANK, (half + 1) * BANK)
            spread = psum_z.tile([P, BANK], F32, tag="z")
            nc.tensor.matmul(out=spread[:], lhsT=ones[:], rhs=g_bias_as_row[:, cols], start=True, stop=True)
            nc.vector.tensor_scalar(
                out=g_bias_turns[:, cols], in0=spread[:],
                scalar1=1.0 / TURN, scalar2=0.25, op0=ALU.mult, op1=ALU.add,
            )

        def is_w(n):
            return 0 <= n < CHUNKS

        def is_g(n):
            return CHUNKS <= n < 2 * CHUNKS

        def turn(n):
            if is_w(n):
                turn_chunk(w_rows, w_grouped, n, on_vector=False)
            if is_g(n):
                turn_chunk(g_rows, g_grouped, n - CHUNKS, on_vector=False)

        def quantise(n):
            if is_w(n):
                quantise_chunk(w_grouped, w_codes, w_scales, n)
            if is_g(n):
                quantise_chunk(g_grouped, g_codes, g_scales, n - CHUNKS)

        h_turned = {}

        def first_product(n):
            if not (is_w(n) and n % 2 == 1):
                return
            s2 = n // PACK
            if n % PACK == 1:
                bank = psum_h.tile([P, PACK, BATCH], F32)
                h_turned[s2] = bank
            for i in (n - 1, n):
                multiply(h_turned[s2][:, i % PACK, :], w_codes, w_scales, i, x_codes, x_scales, 0)
            if n % PACK == PACK - 1:
                nc.vector.tensor_tensor(
                    out=h_grouped[:, s2 * K_PASS : (s2 + 1) * K_PASS].rearrange("p (r t) -> p r t", t=PACK),
                    in0=h_turned[s2][:].rearrange("p t r -> p r t"),
                    in1=b_by_partition[:, s2 * PACK : (s2 + 1) * PACK]
                    .unsqueeze(1)
                    .to_broadcast([P, BATCH, PACK]),
                    op=ALU.add,
                )
                nc.vector.quantize_mx(
                    out=h_codes[:, s2 * BATCH : (s2 + 1) * BATCH].bitcast(FP8X4),
                    scales=h_scales[:, s2 * BATCH : (s2 + 1) * BATCH],
                    in_=h_grouped[:, s2 * K_PASS : (s2 + 1) * K_PASS],
                )

        turns = {}
        shifted = {}
        fraction = {}
        cosine = {}
        cosine_size = {}
        sign_plus_one = {}

        def second_product(n):
            if not (is_g(n) and n % 2 == 1):
                return
            z = psum_z.tile([P, PAIR], F32, tag="z")
            for e in range(2):
                multiply(z[:, e * P : (e + 1) * P], h_codes, h_scales, 0, g_codes, g_scales, n - CHUNKS - 1 + e)
            first_column = (n - CHUNKS - 1) * P
            angle = work.tile([P, PAIR], F32)
            nc.vector.scalar_tensor_tensor(
                out=angle[:], in0=z[:], scalar=1.0 / TURN,
                in1=g_bias_turns[:, first_column : first_column + PAIR],
                op0=ALU.mult, op1=ALU.add,
            )
            turns[n] = angle

        def shift(n):
            if n not in turns:
                return
            whole = work.tile([P, PAIR], F32)
            nc.scalar.activation(out=whole[:], in_=turns[n][:], func=ACT.Copy, bias=ROUND, scale=1.0)
            shifted[n] = whole

        def take_off_whole_turns(n):
            if n not in shifted:
                return
            minus_fraction = work.tile([P, PAIR], F32)
            nc.vector.scalar_tensor_tensor(
                out=minus_fraction[:], in0=shifted[n][:], scalar=ROUND, in1=turns[n][:],
                op0=ALU.subtract, op1=ALU.subtract,
            )
            fraction[n] = minus_fraction

        def sine(n):
            if n not in fraction:
                return
            c = work.tile([P, PAIR], F32)
            nc.scalar.activation(out=c[:], in_=fraction[n][:], func=ACT.Sin, scale=-TURN)
            cosine[n] = c

        def size(n):
            if n not in cosine:
                return
            c_size = work.tile([P, PAIR], F32)
            nc.scalar.activation(out=c_size[:], in_=cosine[n][:], func=ACT.Abs)
            cosine_size[n] = c_size

        def compare(n):
            if n not in cosine_size:
                return
            stays = work.tile([P, PAIR], F32)
            nc.vector.tensor_scalar(
                out=stays[:], in0=cosine_size[n][:], scalar1=EPS, scalar2=2.0, op0=ALU.is_ge, op1=ALU.mult
            )
            sign_plus_one[n] = stays

        def flip(n):
            if n not in sign_plus_one:
                return
            first_column = (n - CHUNKS - 1) * P
            flipped = work.tile([P, PAIR], F32)
            nc.vector.scalar_tensor_tensor(
                out=flipped[:], in0=sign_plus_one[n][:], scalar=1.0, in1=cosine[n][:],
                op0=ALU.subtract, op1=ALU.mult,
            )
            nc.sync.dma_start(out=out[:, first_column : first_column + PAIR], in_=flipped[:])

        pair_stages = (second_product, shift, take_off_whole_turns, sine, size, compare, flip)
        for step in range(2 * CHUNKS + SECOND_PRODUCT_LAG + PAIR_STEPS * (len(pair_stages) - 1)):
            turn(step)
            quantise(step - QUANTISE_LAG)
            first_product(step - FIRST_PRODUCT_LAG)
            for depth, stage in enumerate(pair_stages):
                stage(step - SECOND_PRODUCT_LAG - PAIR_STEPS * depth)
